import numpy as np
import ml_dtypes


def mxq(x, axis, fmt="e4m3"):
    dtype, down = {"e4m3": (ml_dtypes.float8_e4m3fn, 7), "e5m2": (ml_dtypes.float8_e5m2, 14)}[fmt]
    v = np.moveaxis(np.asarray(x, np.float32).astype(ml_dtypes.bfloat16).astype(np.float64), axis, -1)
    blocks = v.reshape(v.shape[:-1] + (-1, 32))
    amax = np.abs(blocks).max(-1, keepdims=True)
    byte = np.maximum(np.where(amax > 0, np.frexp(amax)[1] - 1 + 127, 0) - down, 1)
    scale = np.exp2(byte - 127.0)
    codes = (blocks / scale).astype(np.float32).astype(dtype).astype(np.float64)
    return np.moveaxis((codes * scale).reshape(v.shape), -1, axis)


WIDE = False


def mx_kscale(k):
    if not WIDE:
        return np.ones(k)
    levels = np.array([10, -10, 5, -5, 0])
    a = np.random.permutation(np.resize(levels, k // 512 * 4)).reshape(k // 512, 4)
    idx = np.arange(k)
    return np.exp2(a[idx // 512, idx % 128 // 32])


BF16 = ml_dtypes.bfloat16


def bf(x):
    return np.asarray(x, np.float32).astype(BF16)


def f64(x):
    return np.asarray(x).astype(np.float64)


B, DI, DH = 256, 16384, 128


def sigmoid(v):
    return 1.0 / (1.0 + np.exp(-v))


def setup_inputs():
    s = mx_kscale(DI)
    n = np.random.standard_normal
    a, c = 0.7 / np.sqrt(DI), 0.7 / np.sqrt(DH)
    keep = np.random.uniform(size=B) < 0.9
    return {
        "x": bf(n((B, DI)) * s),
        "h_minors": bf(n((B, DH))),
        "c_minors": bf(n((B, DH))),
        "s0": bf(n((B, DH))),
        "s1": bf(n((B, DH))),
        "s2": bf(n((B, DH))),
        "mask": bf(keep * (0.5 + 0.5 * np.random.uniform(size=B))),
        "weight_ih": bf(n((7 * DH, DI)) * a / s),
        "bias_ih": bf(n(7 * DH) * 0.3),
        "weight_hh": bf(n((4 * DH, DH)) * c),
        "bias_hh": bf(n(4 * DH) * 0.3),
        "weight_sh0": bf(n((DH, DH)) * c),
        "bias_sh0": bf(n(DH) * 0.3),
        "weight_sh1": bf(n((DH, DH)) * c),
        "bias_sh1": bf(n(DH) * 0.3),
        "weight_sh2": bf(n((DH, DH)) * c),
        "bias_sh2": bf(n(DH) * 0.3),
    }


def reference(x, h_minors, c_minors, s0, s1, s2, mask, weight_ih, bias_ih, weight_hh, bias_hh,
              weight_sh0, bias_sh0, weight_sh1, bias_sh1, weight_sh2, bias_sh2):
    d = DH
    m = f64(mask)[:, None]

    tmp = (mxq(f64(x), 1, "e4m3") @ mxq(f64(weight_ih), 1, "e4m3").T) + f64(bias_ih)
    tmp2 = f64(h_minors) @ f64(weight_hh).T + f64(bias_hh)
    tmp3 = np.concatenate([
        f64(s0) @ f64(weight_sh0).T + f64(bias_sh0),
        f64(s1) @ f64(weight_sh1).T + f64(bias_sh1),
        f64(s2) @ f64(weight_sh2).T + f64(bias_sh2),
    ], axis=1)

    tmp_in, tmp_s = tmp[:, :4 * d], tmp[:, 4 * d:]
    pre = tmp_in + tmp2
    ifo = sigmoid(pre[:, :3 * d])
    c_hat = pre[:, 3 * d:]
    i_g, f_g, o_g = ifo[:, :d], ifo[:, d:2 * d], ifo[:, 2 * d:]

    c_t = (f_g * f64(c_minors) + i_g * np.tanh(c_hat)) * m
    tc = np.tanh(c_t) * m
    h = o_g * tc

    bg = sigmoid(tmp_s + tmp3)
    b0, b1, b2 = bg[:, :d], bg[:, d:2 * d], bg[:, 2 * d:]

    s_0 = (b0 + 1.0 - o_g) * tc
    s_1 = (b1 + 2.0 - o_g - s_0) * 0.5 * tc
    s_2 = (b2 + 3.0 - o_g - (2.0 * s_0 + s_1)) * (1.0 / 3.0) * tc

    return (h, c_t, s_0, s_1, s_2)

@@ -1,0 +1,317 @@
+from contextlib import ExitStack
+
+import concourse.mybir as mybir
+from concourse.masks import make_identity
+
+F32 = mybir.dt.float32
+BF16 = mybir.dt.bfloat16
+I32 = mybir.dt.int32
+U32 = mybir.dt.uint32
+U8 = mybir.dt.uint8
+FP8X4 = mybir.dt.float8_e4m3fn_x4
+ALU = mybir.AluOpType
+ACT = mybir.ActivationFunctionType
+
+P = 128
+BATCH, D_IN, D_HID = 256, 16384, 128
+GATES = 7 * D_HID
+LSTM_GATES = 4 * D_HID
+
+PACK = 4
+K_PASS = P * PACK
+N_PASSES = D_IN // K_PASS
+HALVES = 2
+
+X_TILES = BATCH // P
+W_TILES = GATES // P
+ROW_TILES = X_TILES + W_TILES
+ROWS = ROW_TILES * P
+N_MOVING = 512
+COLS = X_TILES * P + 2 * N_MOVING
+
+PASSES_PER_ROUND = 2
+ROUND_K = PASSES_PER_ROUND * K_PASS
+ROUNDS = D_IN // ROUND_K
+SLAB_K = 2048
+ROUNDS_PER_SLAB = SLAB_K // ROUND_K
+SLABS = D_IN // SLAB_K
+RAW_SLABS = 3
+WIDE_ROWS = 1024
+
+FLOPS = 2 * BATCH * GATES * D_IN + 2 * BATCH * GATES * D_HID
+
+
+def tile_share_lstm_cell_pa_k_kernel(
+    tc, x, h_minors, c_minors, s0, s1, s2, mask, weight_ih, bias_ih, weight_hh, bias_hh,
+    weight_sh0, bias_sh0, weight_sh1, bias_sh1, weight_sh2, bias_sh2,
+    out_0, out_1, out_2, out_3, out_4,
+):
+    nc = tc.nc
+    with ExitStack() as ctx:
+        ctx.enter_context(tc.manual_schedule())
+        const = ctx.enter_context(tc.tile_pool(name="const", bufs=1))
+        raw_pool = ctx.enter_context(tc.tile_pool(name="raw", bufs=RAW_SLABS * ROW_TILES))
+        grouped_pool = ctx.enter_context(tc.tile_pool(name="grouped", bufs=2))
+        tail = ctx.enter_context(tc.tile_pool(name="tail", bufs=1))
+        acc_pool = ctx.enter_context(tc.psum_pool(name="acc", bufs=1))
+        bank_pool = ctx.enter_context(tc.psum_pool(name="bank", bufs=4))
+
+        def load_slab(s):
+            k_cols = slice(s * SLAB_K, (s + 1) * SLAB_K)
+            tiles = []
+            for rt in range(ROW_TILES):
+                raw = raw_pool.tile([P, SLAB_K], BF16, tag="raw")
+                if rt < X_TILES:
+                    rows = x[rt * P : (rt + 1) * P, k_cols]
+                else:
+                    rows = weight_ih[(rt - X_TILES) * P : (rt - X_TILES + 1) * P, k_cols]
+                nc.sync.dma_start(out=raw[:], in_=rows)
+                tiles.append(raw)
+            return tiles
+
+        slabs = {}
+        for s in range(RAW_SLABS):
+            slabs[s] = load_slab(s)
+
+        ident_f32 = const.tile([P, P], F32)
+        make_identity(nc, ident_f32[:])
+        ident_bf16 = const.tile([P, P], BF16)
+        make_identity(nc, ident_bf16[:])
+        ones = const.tile([P, P], BF16)
+        nc.vector.memset(ones[:], 1.0)
+        warm = const.tile([P, 1], F32)
+        nc.vector.memset(warm[:], 0.0)
+        nc.scalar.activation(out=warm[:], in_=warm[:], func=ACT.Sigmoid)
+
+        mx_tiles = []
+        for n in range(2):
+            codes = const.tile([P, PASSES_PER_ROUND * COLS], U32, name="codes%d" % n, align_bytes=64)
+            scales = const.tile([P, PASSES_PER_ROUND * COLS], U8, name="scales%d" % n, align_bytes=64)
+            for a in range(PASSES_PER_ROUND):
+                fill = slice(a * COLS + ROWS, (a + 1) * COLS)
+                nc.vector.memset(codes[:, fill].bitcast(I32), 0)
+                nc.vector.memset(scales[:, fill].bitcast(I32), 0)
+            mx_tiles.append((codes, scales))
+
+        act_raw = const.tile([P, 4, X_TILES, D_HID], BF16)
+        for j, act in enumerate((h_minors, s0, s1, s2)):
+            nc.gpsimd.dma_start(out=act_raw[:, j, :, :], in_=act.rearrange("(t p) d -> p t d", p=P))
+        w_raw = const.tile([P, 8, D_HID], BF16)
+        nc.vector.memset(w_raw[:, 7, :], 0.0)
+        nc.gpsimd.dma_start(out=w_raw[:, 0:4, :], in_=weight_hh.rearrange("(j p) d -> p j d", p=P))
+        for j, w_sh in enumerate((weight_sh0, weight_sh1, weight_sh2)):
+            nc.gpsimd.dma_start(out=w_raw[:, 4 + j, :], in_=w_sh)
+        nc.gpsimd.dma_start(out=w_raw[0:X_TILES, 7, :], in_=mask.rearrange("(t p) -> t p", p=P))
+        bias_rows = const.tile([P, GATES], BF16)
+        nc.vector.memset(bias_rows[:], 0.0)
+        nc.gpsimd.dma_start(out=bias_rows[0:1, :], in_=bias_ih.rearrange("(o n) -> o n", o=1))
+        nc.gpsimd.dma_start(
+            out=bias_rows[1:2, 0:LSTM_GATES], in_=bias_hh.rearrange("(o n) -> o n", o=1)
+        )
+        for j, b_sh in enumerate((bias_sh0, bias_sh1, bias_sh2)):
+            cols = slice(LSTM_GATES + j * D_HID, LSTM_GATES + (j + 1) * D_HID)
+            nc.gpsimd.dma_start(out=bias_rows[1:2, cols], in_=b_sh.rearrange("(o n) -> o n", o=1))
+        c_raw = const.tile([P, X_TILES, D_HID], BF16)
+        nc.gpsimd.dma_start(out=c_raw[:], in_=c_minors.rearrange("(t p) d -> p t d", p=P))
+
+        grouped_of = {}
+
+        def transpose_round(i):
+            s, r = divmod(i, ROUNDS_PER_SLAB)
+            first_word = r * ROUND_K // 2
+            grouped = grouped_pool.tile(
+                [P, PASSES_PER_ROUND * ROWS * PACK], BF16, tag="grouped", align_bytes=64
+            )
+            grouped_words = grouped[:].bitcast(F32).rearrange(
+                "p (a r u) -> p a r u", a=PASSES_PER_ROUND, u=HALVES
+            )
+            for rt in range(ROW_TILES):
+                words = slabs[s][rt][:].bitcast(F32)
+                bank = bank_pool.tile([P, PASSES_PER_ROUND, HALVES, P], F32, tag="bank")
+                for a in range(PASSES_PER_ROUND):
+                    for u in range(HALVES):
+                        w0 = first_word + (a * HALVES + u) * P
+                        nc.tensor.transpose(bank[:, a, u, :], words[:, w0 : w0 + P], ident_f32[:])
+                dst = grouped_words[:, :, rt * P : (rt + 1) * P, :]
+                src = bank[:].rearrange("p a u r -> p a r u")
+                if rt % 4 == 3:
+                    nc.vector.tensor_copy(out=dst, in_=src)
+                else:
+                    nc.scalar.copy(out=dst, in_=src)
+            grouped_of[i] = grouped
+            if r == ROUNDS_PER_SLAB - 1 and s + RAW_SLABS < SLABS:
+                slabs[s + RAW_SLABS] = load_slab(s + RAW_SLABS)
+
+        def quantise_round(i):
+            codes, scales = mx_tiles[i % 2]
+            grouped = grouped_of[i]
+            for lo, hi in ((0, WIDE_ROWS), (WIDE_ROWS, ROWS)):
+                for a in range(PASSES_PER_ROUND):
+                    nc.vector.quantize_mx(
+                        out=codes[:, a * COLS + lo : a * COLS + hi].bitcast(FP8X4),
+                        scales=scales[:, a * COLS + lo : a * COLS + hi],
+                        in_=grouped[:, (a * ROWS + lo) * PACK : (a * ROWS + hi) * PACK],
+                    )
+
+        acc = [
+            [acc_pool.tile([P, N_MOVING], F32, name="acc%d%d" % (bt, n)) for n in range(2)]
+            for bt in range(X_TILES)
+        ]
+
+        def multiply_round(i):
+            codes, scales = mx_tiles[i % 2]
+            for a in range(PASSES_PER_ROUND):
+                c = i * PASSES_PER_ROUND + a
+                for bt in range(X_TILES):
+                    x_cols = slice(a * COLS + bt * P, a * COLS + (bt + 1) * P)
+                    for n in range(2):
+                        w0 = a * COLS + X_TILES * P + n * N_MOVING
+                        w_cols = slice(w0, w0 + N_MOVING)
+                        nc.tensor.matmul_mx(
+                            out=acc[bt][n][:],
+                            lhsT=codes[:, x_cols].bitcast(FP8X4),
+                            lhsT_scale=scales[:, x_cols],
+                            rhs=codes[:, w_cols].bitcast(FP8X4),
+                            rhs_scale=scales[:, w_cols],
+                            start=(c == 0),
+                            stop=(c == N_PASSES - 1),
+                        )
+
+        addend = const.tile([P, X_TILES, GATES], F32)
+        mask_col = const.tile([P, X_TILES], F32)
+        c_masked = const.tile([P, X_TILES, D_HID], F32)
+
+        def small_products():
+            act_t_bank = bank_pool.tile([P, 4 * X_TILES, P], BF16, tag="bank")
+            for j in range(4):
+                for bt in range(X_TILES):
+                    nc.tensor.transpose(
+                        act_t_bank[:, j * X_TILES + bt, :], act_raw[:, j, bt, :], ident_bf16[:]
+                    )
+            act_t = const.tile([P, 4 * X_TILES, P], BF16)
+            nc.vector.tensor_copy(out=act_t[:], in_=act_t_bank[:])
+            w_t_bank = bank_pool.tile([P, 8 * D_HID], BF16, tag="bank")
+            for j in range(8):
+                nc.tensor.transpose(
+                    w_t_bank[:, j * D_HID : (j + 1) * D_HID], w_raw[:, j, :], ident_bf16[:]
+                )
+            w_t = const.tile([P, 8 * D_HID], BF16)
+            nc.scalar.copy(out=w_t[:], in_=w_t_bank[:])
+            nc.vector.tensor_copy(out=mask_col[:], in_=w_t[:, GATES : GATES + X_TILES])
+            for bt in range(X_TILES):
+                nc.vector.tensor_scalar_mul(
+                    out=c_masked[:, bt, :], in0=c_raw[:, bt, :], scalar1=mask_col[:, bt : bt + 1]
+                )
+            for bt in range(X_TILES):
+                lstm = bank_pool.tile([P, LSTM_GATES], F32, tag="bank")
+                nc.tensor.matmul(
+                    out=lstm[:], lhsT=act_t[:, bt, :], rhs=w_t[:, 0:LSTM_GATES],
+                    start=True, stop=False,
+                )
+                nc.tensor.matmul(
+                    out=lstm[:], lhsT=ones[:], rhs=bias_rows[:, 0:LSTM_GATES],
+                    start=False, stop=True,
+                )
+                nc.scalar.copy(out=addend[:, bt, 0:LSTM_GATES], in_=lstm[:])
+                shared = bank_pool.tile([P, GATES - LSTM_GATES], F32, tag="bank")
+                for j in range(3):
+                    cols = slice(LSTM_GATES + j * D_HID, LSTM_GATES + (j + 1) * D_HID)
+                    group = shared[:, j * D_HID : (j + 1) * D_HID]
+                    nc.tensor.matmul(
+                        out=group, lhsT=act_t[:, (1 + j) * X_TILES + bt, :], rhs=w_t[:, cols],
+                        start=True, stop=False,
+                    )
+                    nc.tensor.matmul(
+                        out=group, lhsT=ones[:], rhs=bias_rows[:, cols], start=False, stop=True
+                    )
+                nc.vector.tensor_copy(out=addend[:, bt, LSTM_GATES:GATES], in_=shared[:])
+
+        transpose_round(0)
+        quantise_round(0)
+        transpose_round(1)
+        small_products()
+        multiply_round(0)
+        for i in range(1, ROUNDS):
+            quantise_round(i)
+            if i + 1 < ROUNDS:
+                transpose_round(i + 1)
+            multiply_round(i)
+
+        def block(tile, j):
+            return tile[:, :, j * D_HID : (j + 1) * D_HID]
+
+        pre = tail.tile([P, X_TILES, GATES], F32)
+        gate = tail.tile([P, X_TILES, GATES], F32)
+        for bt in range(X_TILES):
+            nc.vector.tensor_add(
+                out=pre[:, bt, 0:N_MOVING], in0=acc[bt][0][:], in1=addend[:, bt, 0:N_MOVING]
+            )
+        nc.scalar.activation(out=gate[:, :, 0 : 3 * D_HID], in_=pre[:, :, 0 : 3 * D_HID], func=ACT.Sigmoid)
+        nc.scalar.activation(out=block(gate, 3), in_=block(pre, 3), func=ACT.Tanh)
+        for bt in range(X_TILES):
+            nc.vector.tensor_add(
+                out=pre[:, bt, N_MOVING:GATES],
+                in0=acc[bt][1][:, 0 : GATES - N_MOVING],
+                in1=addend[:, bt, N_MOVING:GATES],
+            )
+        nc.scalar.activation(
+            out=gate[:, :, LSTM_GATES:GATES], in_=pre[:, :, LSTM_GATES:GATES], func=ACT.Sigmoid
+        )
+        i_g, f_g, o_g, c_hat = [block(gate, j) for j in range(4)]
+
+        kept = tail.tile([P, X_TILES, D_HID], F32)
+        nc.vector.tensor_mul(out=kept[:], in0=f_g, in1=c_masked[:])
+        fresh = tail.tile([P, X_TILES, D_HID], F32)
+        for bt in range(X_TILES):
+            nc.vector.scalar_tensor_tensor(
+                out=fresh[:, bt, :], in0=i_g[:, bt, :], scalar=mask_col[:, bt : bt + 1],
+                in1=c_hat[:, bt, :], op0=ALU.mult, op1=ALU.mult,
+            )
+        c_t = tail.tile([P, X_TILES, D_HID], F32)
+        nc.vector.tensor_add(out=c_t[:], in0=kept[:], in1=fresh[:])
+        tanh_c = tail.tile([P, X_TILES, D_HID], F32)
+        nc.scalar.activation(out=tanh_c[:], in_=c_t[:], func=ACT.Tanh)
+
+        def store(out, tile):
+            nc.sync.dma_start(out=out.rearrange("(t p) d -> p t d", p=P), in_=tile[:])
+
+        store(out_1, c_t)
+        b_less_o = []
+        for j in range(3):
+            diff = tail.tile([P, X_TILES, D_HID], F32, name="b_less_o%d" % j)
+            nc.vector.tensor_sub(out=diff[:], in0=block(gate, 4 + j), in1=o_g)
+            b_less_o.append(diff)
+        tc_m = tail.tile([P, X_TILES, D_HID], F32)
+        for bt in range(X_TILES):
+            nc.vector.tensor_scalar_mul(
+                out=tc_m[:, bt, :], in0=tanh_c[:, bt, :], scalar1=mask_col[:, bt : bt + 1]
+            )
+        s_0 = tail.tile([P, X_TILES, D_HID], F32)
+        nc.vector.scalar_tensor_tensor(
+            out=s_0[:], in0=b_less_o[0][:], scalar=1.0, in1=tc_m[:], op0=ALU.add, op1=ALU.mult
+        )
+        store(out_2, s_0)
+        h = tail.tile([P, X_TILES, D_HID], F32)
+        nc.vector.tensor_mul(out=h[:], in0=o_g, in1=tc_m[:])
+        store(out_0, h)
+        rest_1 = tail.tile([P, X_TILES, D_HID], F32)
+        nc.vector.scalar_tensor_tensor(
+            out=rest_1[:], in0=b_less_o[1][:], scalar=2.0, in1=s_0[:], op0=ALU.add, op1=ALU.subtract
+        )
+        rest_2 = tail.tile([P, X_TILES, D_HID], F32)
+        nc.vector.scalar_tensor_tensor(
+            out=rest_2[:], in0=s_0[:], scalar=-2.0, in1=b_less_o[2][:], op0=ALU.mult, op1=ALU.add
+        )
+        s_1 = tail.tile([P, X_TILES, D_HID], F32)
+        nc.vector.scalar_tensor_tensor(
+            out=s_1[:], in0=rest_1[:], scalar=0.5, in1=tc_m[:], op0=ALU.mult, op1=ALU.mult
+        )
+        store(out_3, s_1)
+        nc.vector.scalar_tensor_tensor(
+            out=rest_2[:], in0=rest_2[:], scalar=3.0, in1=s_1[:], op0=ALU.add, op1=ALU.subtract
+        )
+        s_2 = tail.tile([P, X_TILES, D_HID], F32)
+        nc.vector.scalar_tensor_tensor(
+            out=s_2[:], in0=rest_2[:], scalar=1.0 / 3.0, in1=tc_m[:], op0=ALU.mult, op1=ALU.mult
+        )
+        store(out_4, s_2)

@@ -36,7 +36,10 @@ SLAB_K = 2048
 ROUNDS_PER_SLAB = SLAB_K // ROUND_K
 SLABS = D_IN // SLAB_K
 RAW_SLABS = 3
-WIDE_ROWS = 1024
+T_BANKS = 4
+RUN_TILES = (range(0, T_BANKS), range(T_BANKS, ROW_TILES))
+RUN_ROWS = (((0, 512),), ((512, 1024), (1024, ROWS)))
+SMALL_PRODUCTS_ROUND = 0
 
 FLOPS = 2 * BATCH * GATES * D_IN + 2 * BATCH * GATES * D_HID
 
@@ -54,24 +57,27 @@ def tile_share_lstm_cell_pa_k_kernel(
         grouped_pool = ctx.enter_context(tc.tile_pool(name="grouped", bufs=2))
         tail = ctx.enter_context(tc.tile_pool(name="tail", bufs=1))
         acc_pool = ctx.enter_context(tc.psum_pool(name="acc", bufs=1))
-        bank_pool = ctx.enter_context(tc.psum_pool(name="bank", bufs=4))
+        bank_pool = ctx.enter_context(tc.psum_pool(name="bank", bufs=T_BANKS))
 
-        def load_slab(s):
-            k_cols = slice(s * SLAB_K, (s + 1) * SLAB_K)
+        def load_slab(s, cuts):
             tiles = []
             for rt in range(ROW_TILES):
                 raw = raw_pool.tile([P, SLAB_K], BF16, tag="raw")
-                if rt < X_TILES:
-                    rows = x[rt * P : (rt + 1) * P, k_cols]
-                else:
-                    rows = weight_ih[(rt - X_TILES) * P : (rt - X_TILES + 1) * P, k_cols]
-                nc.sync.dma_start(out=raw[:], in_=rows)
                 tiles.append(raw)
+            width = SLAB_K // cuts
+            for cut in range(cuts):
+                k_cols = slice(s * SLAB_K + cut * width, s * SLAB_K + (cut + 1) * width)
+                for rt in range(ROW_TILES):
+                    if rt < X_TILES:
+                        rows = x[rt * P : (rt + 1) * P, k_cols]
+                    else:
+                        rows = weight_ih[(rt - X_TILES) * P : (rt - X_TILES + 1) * P, k_cols]
+                    nc.sync.dma_start(out=tiles[rt][:, cut * width : (cut + 1) * width], in_=rows)
             return tiles
 
-        slabs = {}
-        for s in range(RAW_SLABS):
-            slabs[s] = load_slab(s)
+        slabs = {0: load_slab(0, ROUNDS_PER_SLAB)}
+        for s in range(1, RAW_SLABS):
+            slabs[s] = load_slab(s, 1)
 
         ident_f32 = const.tile([P, P], F32)
         make_identity(nc, ident_f32[:])
@@ -116,16 +122,19 @@ def tile_share_lstm_cell_pa_k_kernel(
 
         grouped_of = {}
 
-        def transpose_round(i):
+        def prepare(i, run):
             s, r = divmod(i, ROUNDS_PER_SLAB)
             first_word = r * ROUND_K // 2
-            grouped = grouped_pool.tile(
-                [P, PASSES_PER_ROUND * ROWS * PACK], BF16, tag="grouped", align_bytes=64
-            )
+            if run == 0:
+                grouped_of[i] = grouped_pool.tile(
+                    [P, PASSES_PER_ROUND * ROWS * PACK], BF16,
+                    name="grouped", tag="grouped", align_bytes=64,
+                )
+            grouped = grouped_of[i]
             grouped_words = grouped[:].bitcast(F32).rearrange(
                 "p (a r u) -> p a r u", a=PASSES_PER_ROUND, u=HALVES
             )
-            for rt in range(ROW_TILES):
+            for rt in RUN_TILES[run]:
                 words = slabs[s][rt][:].bitcast(F32)
                 bank = bank_pool.tile([P, PASSES_PER_ROUND, HALVES, P], F32, tag="bank")
                 for a in range(PASSES_PER_ROUND):
@@ -134,18 +143,14 @@ def tile_share_lstm_cell_pa_k_kernel(
                         nc.tensor.transpose(bank[:, a, u, :], words[:, w0 : w0 + P], ident_f32[:])
                 dst = grouped_words[:, :, rt * P : (rt + 1) * P, :]
                 src = bank[:].rearrange("p a u r -> p a r u")
-                if rt % 4 == 3:
+                if rt % T_BANKS == 2:
                     nc.vector.tensor_copy(out=dst, in_=src)
                 else:
                     nc.scalar.copy(out=dst, in_=src)
-            grouped_of[i] = grouped
-            if r == ROUNDS_PER_SLAB - 1 and s + RAW_SLABS < SLABS:
-                slabs[s + RAW_SLABS] = load_slab(s + RAW_SLABS)
-
-        def quantise_round(i):
+            if run == 1 and r == ROUNDS_PER_SLAB - 1 and s + RAW_SLABS < SLABS:
+                slabs[s + RAW_SLABS] = load_slab(s + RAW_SLABS, 1)
             codes, scales = mx_tiles[i % 2]
-            grouped = grouped_of[i]
-            for lo, hi in ((0, WIDE_ROWS), (WIDE_ROWS, ROWS)):
+            for lo, hi in RUN_ROWS[run]:
                 for a in range(PASSES_PER_ROUND):
                     nc.vector.quantize_mx(
                         out=codes[:, a * COLS + lo : a * COLS + hi].bitcast(FP8X4),
@@ -158,24 +163,23 @@ def tile_share_lstm_cell_pa_k_kernel(
             for bt in range(X_TILES)
         ]
 
-        def multiply_round(i):
+        def multiply_pass(i, a):
             codes, scales = mx_tiles[i % 2]
-            for a in range(PASSES_PER_ROUND):
-                c = i * PASSES_PER_ROUND + a
-                for bt in range(X_TILES):
-                    x_cols = slice(a * COLS + bt * P, a * COLS + (bt + 1) * P)
-                    for n in range(2):
-                        w0 = a * COLS + X_TILES * P + n * N_MOVING
-                        w_cols = slice(w0, w0 + N_MOVING)
-                        nc.tensor.matmul_mx(
-                            out=acc[bt][n][:],
-                            lhsT=codes[:, x_cols].bitcast(FP8X4),
-                            lhsT_scale=scales[:, x_cols],
-                            rhs=codes[:, w_cols].bitcast(FP8X4),
-                            rhs_scale=scales[:, w_cols],
-                            start=(c == 0),
-                            stop=(c == N_PASSES - 1),
-                        )
+            c = i * PASSES_PER_ROUND + a
+            for bt in range(X_TILES):
+                x_cols = slice(a * COLS + bt * P, a * COLS + (bt + 1) * P)
+                for n in range(2):
+                    w0 = a * COLS + X_TILES * P + n * N_MOVING
+                    w_cols = slice(w0, w0 + N_MOVING)
+                    nc.tensor.matmul_mx(
+                        out=acc[bt][n][:],
+                        lhsT=codes[:, x_cols].bitcast(FP8X4),
+                        lhsT_scale=scales[:, x_cols],
+                        rhs=codes[:, w_cols].bitcast(FP8X4),
+                        rhs_scale=scales[:, w_cols],
+                        start=(c == 0),
+                        stop=(c == N_PASSES - 1),
+                    )
 
         addend = const.tile([P, X_TILES, GATES], F32)
         mask_col = const.tile([P, X_TILES], F32)
@@ -226,16 +230,15 @@ def tile_share_lstm_cell_pa_k_kernel(
                     )
                 nc.vector.tensor_copy(out=addend[:, bt, LSTM_GATES:GATES], in_=shared[:])
 
-        transpose_round(0)
-        quantise_round(0)
-        transpose_round(1)
-        small_products()
-        multiply_round(0)
-        for i in range(1, ROUNDS):
-            quantise_round(i)
-            if i + 1 < ROUNDS:
-                transpose_round(i + 1)
-            multiply_round(i)
+        for run in range(PASSES_PER_ROUND):
+            prepare(0, run)
+        for i in range(ROUNDS):
+            for a in range(PASSES_PER_ROUND):
+                if i + 1 < ROUNDS:
+                    prepare(i + 1, a)
+                multiply_pass(i, a)
+            if i == SMALL_PRODUCTS_ROUND:
+                small_products()
 
         def block(tile, j):
             return tile[:, :, j * D_HID : (j + 1) * D_HID]

@@ -35,11 +35,15 @@ ROUNDS = D_IN // ROUND_K
 SLAB_K = 2048
 ROUNDS_PER_SLAB = SLAB_K // ROUND_K
 SLABS = D_IN // SLAB_K
-RAW_SLABS = 3
+RAW_SLABS = 2
 T_BANKS = 4
-RUN_TILES = (range(0, T_BANKS), range(T_BANKS, ROW_TILES))
-RUN_ROWS = (((0, 512),), ((512, 1024), (1024, ROWS)))
-SMALL_PRODUCTS_ROUND = 0
+RUNS_PER_ROUND = 3
+RUN_TILES = ROW_TILES // RUNS_PER_ROUND
+N_RUNS = ROUNDS * RUNS_PER_ROUND
+RUN_ROWS = (((0, 256),), ((256, 768),), ((768, 1024), (1024, ROWS)))
+LAG = 5
+MX_BUFS = 3
+SMALL_PRODUCTS_AFTER_RUN = 7
 
 FLOPS = 2 * BATCH * GATES * D_IN + 2 * BATCH * GATES * D_HID
 
@@ -59,25 +63,25 @@ def tile_share_lstm_cell_pa_k_kernel(
         acc_pool = ctx.enter_context(tc.psum_pool(name="acc", bufs=1))
         bank_pool = ctx.enter_context(tc.psum_pool(name="bank", bufs=T_BANKS))
 
-        def load_slab(s, cuts):
-            tiles = []
-            for rt in range(ROW_TILES):
-                raw = raw_pool.tile([P, SLAB_K], BF16, tag="raw")
-                tiles.append(raw)
-            width = SLAB_K // cuts
-            for cut in range(cuts):
-                k_cols = slice(s * SLAB_K + cut * width, s * SLAB_K + (cut + 1) * width)
-                for rt in range(ROW_TILES):
-                    if rt < X_TILES:
-                        rows = x[rt * P : (rt + 1) * P, k_cols]
-                    else:
-                        rows = weight_ih[(rt - X_TILES) * P : (rt - X_TILES + 1) * P, k_cols]
-                    nc.sync.dma_start(out=tiles[rt][:, cut * width : (cut + 1) * width], in_=rows)
-            return tiles
+        raw_of = {}
 
-        slabs = {0: load_slab(0, ROUNDS_PER_SLAB)}
+        def load(s, rt, cut, cuts):
+            if cut == 0:
+                raw_of[(s, rt)] = raw_pool.tile([P, SLAB_K], BF16, name="raw", tag="raw")
+            width = SLAB_K // cuts
+            k_cols = slice(s * SLAB_K + cut * width, s * SLAB_K + (cut + 1) * width)
+            if rt < X_TILES:
+                rows = x[rt * P : (rt + 1) * P, k_cols]
+            else:
+                rows = weight_ih[(rt - X_TILES) * P : (rt - X_TILES + 1) * P, k_cols]
+            nc.sync.dma_start(out=raw_of[(s, rt)][:, cut * width : (cut + 1) * width], in_=rows)
+
+        for cut in range(ROUNDS_PER_SLAB):
+            for rt in range(ROW_TILES):
+                load(0, rt, cut, ROUNDS_PER_SLAB)
         for s in range(1, RAW_SLABS):
-            slabs[s] = load_slab(s, 1)
+            for rt in range(ROW_TILES):
+                load(s, rt, 0, 1)
 
         ident_f32 = const.tile([P, P], F32)
         make_identity(nc, ident_f32[:])
@@ -90,7 +94,7 @@ def tile_share_lstm_cell_pa_k_kernel(
         nc.scalar.activation(out=warm[:], in_=warm[:], func=ACT.Sigmoid)
 
         mx_tiles = []
-        for n in range(2):
+        for n in range(MX_BUFS):
             codes = const.tile([P, PASSES_PER_ROUND * COLS], U32, name="codes%d" % n, align_bytes=64)
             scales = const.tile([P, PASSES_PER_ROUND * COLS], U8, name="scales%d" % n, align_bytes=64)
             for a in range(PASSES_PER_ROUND):
@@ -122,7 +126,7 @@ def tile_share_lstm_cell_pa_k_kernel(
 
         grouped_of = {}
 
-        def prepare(i, run):
+        def transpose_run(i, run):
             s, r = divmod(i, ROUNDS_PER_SLAB)
             first_word = r * ROUND_K // 2
             if run == 0:
@@ -130,12 +134,11 @@ def tile_share_lstm_cell_pa_k_kernel(
                     [P, PASSES_PER_ROUND * ROWS * PACK], BF16,
                     name="grouped", tag="grouped", align_bytes=64,
                 )
-            grouped = grouped_of[i]
-            grouped_words = grouped[:].bitcast(F32).rearrange(
+            grouped_words = grouped_of[i][:].bitcast(F32).rearrange(
                 "p (a r u) -> p a r u", a=PASSES_PER_ROUND, u=HALVES
             )
-            for rt in RUN_TILES[run]:
-                words = slabs[s][rt][:].bitcast(F32)
+            for rt in range(run * RUN_TILES, (run + 1) * RUN_TILES):
+                words = raw_of[(s, rt)][:].bitcast(F32)
                 bank = bank_pool.tile([P, PASSES_PER_ROUND, HALVES, P], F32, tag="bank")
                 for a in range(PASSES_PER_ROUND):
                     for u in range(HALVES):
@@ -143,19 +146,21 @@ def tile_share_lstm_cell_pa_k_kernel(
                         nc.tensor.transpose(bank[:, a, u, :], words[:, w0 : w0 + P], ident_f32[:])
                 dst = grouped_words[:, :, rt * P : (rt + 1) * P, :]
                 src = bank[:].rearrange("p a u r -> p a r u")
-                if rt % T_BANKS == 2:
+                if rt % RUN_TILES == 1:
                     nc.vector.tensor_copy(out=dst, in_=src)
                 else:
                     nc.scalar.copy(out=dst, in_=src)
-            if run == 1 and r == ROUNDS_PER_SLAB - 1 and s + RAW_SLABS < SLABS:
-                slabs[s + RAW_SLABS] = load_slab(s + RAW_SLABS, 1)
-            codes, scales = mx_tiles[i % 2]
+                if r == ROUNDS_PER_SLAB - 1 and s + RAW_SLABS < SLABS:
+                    load(s + RAW_SLABS, rt, 0, 1)
+
+        def quantise_run(i, run):
+            codes, scales = mx_tiles[i % MX_BUFS]
             for lo, hi in RUN_ROWS[run]:
                 for a in range(PASSES_PER_ROUND):
                     nc.vector.quantize_mx(
                         out=codes[:, a * COLS + lo : a * COLS + hi].bitcast(FP8X4),
                         scales=scales[:, a * COLS + lo : a * COLS + hi],
-                        in_=grouped[:, (a * ROWS + lo) * PACK : (a * ROWS + hi) * PACK],
+                        in_=grouped_of[i][:, (a * ROWS + lo) * PACK : (a * ROWS + hi) * PACK],
                     )
 
         acc = [
@@ -163,23 +168,27 @@ def tile_share_lstm_cell_pa_k_kernel(
             for bt in range(X_TILES)
         ]
 
-        def multiply_pass(i, a):
-            codes, scales = mx_tiles[i % 2]
-            c = i * PASSES_PER_ROUND + a
-            for bt in range(X_TILES):
+        round_matmuls = [
+            (a, bt, n) for a in range(PASSES_PER_ROUND) for bt in range(X_TILES) for n in range(2)
+        ]
+        per_run = -(-len(round_matmuls) // RUNS_PER_ROUND)
+
+        def multiply_run(i, run):
+            codes, scales = mx_tiles[i % MX_BUFS]
+            for a, bt, n in round_matmuls[run * per_run : (run + 1) * per_run]:
+                c = i * PASSES_PER_ROUND + a
                 x_cols = slice(a * COLS + bt * P, a * COLS + (bt + 1) * P)
-                for n in range(2):
-                    w0 = a * COLS + X_TILES * P + n * N_MOVING
-                    w_cols = slice(w0, w0 + N_MOVING)
-                    nc.tensor.matmul_mx(
-                        out=acc[bt][n][:],
-                        lhsT=codes[:, x_cols].bitcast(FP8X4),
-                        lhsT_scale=scales[:, x_cols],
-                        rhs=codes[:, w_cols].bitcast(FP8X4),
-                        rhs_scale=scales[:, w_cols],
-                        start=(c == 0),
-                        stop=(c == N_PASSES - 1),
-                    )
+                w0 = a * COLS + X_TILES * P + n * N_MOVING
+                w_cols = slice(w0, w0 + N_MOVING)
+                nc.tensor.matmul_mx(
+                    out=acc[bt][n][:],
+                    lhsT=codes[:, x_cols].bitcast(FP8X4),
+                    lhsT_scale=scales[:, x_cols],
+                    rhs=codes[:, w_cols].bitcast(FP8X4),
+                    rhs_scale=scales[:, w_cols],
+                    start=(c == 0),
+                    stop=(c == N_PASSES - 1),
+                )
 
         addend = const.tile([P, X_TILES, GATES], F32)
         mask_col = const.tile([P, X_TILES], F32)
@@ -230,14 +239,14 @@ def tile_share_lstm_cell_pa_k_kernel(
                     )
                 nc.vector.tensor_copy(out=addend[:, bt, LSTM_GATES:GATES], in_=shared[:])
 
-        for run in range(PASSES_PER_ROUND):
-            prepare(0, run)
-        for i in range(ROUNDS):
-            for a in range(PASSES_PER_ROUND):
-                if i + 1 < ROUNDS:
-                    prepare(i + 1, a)
-                multiply_pass(i, a)
-            if i == SMALL_PRODUCTS_ROUND:
+        for turn in range(N_RUNS + LAG):
+            if turn < N_RUNS:
+                transpose_run(turn // RUNS_PER_ROUND, turn % RUNS_PER_ROUND)
+            if 1 <= turn <= N_RUNS:
+                quantise_run((turn - 1) // RUNS_PER_ROUND, (turn - 1) % RUNS_PER_ROUND)
+            if turn >= LAG:
+                multiply_run((turn - LAG) // RUNS_PER_ROUND, (turn - LAG) % RUNS_PER_ROUND)
+            if turn == SMALL_PRODUCTS_AFTER_RUN:
                 small_products()
 
         def block(tile, j):

@@ -40,8 +40,8 @@ T_BANKS = 4
 RUNS_PER_ROUND = 3
 RUN_TILES = ROW_TILES // RUNS_PER_ROUND
 N_RUNS = ROUNDS * RUNS_PER_ROUND
-RUN_ROWS = (((0, 256),), ((256, 768),), ((768, 1024), (1024, ROWS)))
-LAG = 5
+RUN_CUTS = ((0, 2 * P), (2 * P, 3 * P))
+LAG = 4
 MX_BUFS = 3
 SMALL_PRODUCTS_AFTER_RUN = 7
 
@@ -155,7 +155,9 @@ def tile_share_lstm_cell_pa_k_kernel(
 
         def quantise_run(i, run):
             codes, scales = mx_tiles[i % MX_BUFS]
-            for lo, hi in RUN_ROWS[run]:
+            first_row = run * RUN_TILES * P
+            for cut_lo, cut_hi in RUN_CUTS:
+                lo, hi = first_row + cut_lo, first_row + cut_hi
                 for a in range(PASSES_PER_ROUND):
                     nc.vector.quantize_mx(
                         out=codes[:, a * COLS + lo : a * COLS + hi].bitcast(FP8X4),
@@ -169,13 +171,13 @@ def tile_share_lstm_cell_pa_k_kernel(
         ]
 
         round_matmuls = [
-            (a, bt, n) for a in range(PASSES_PER_ROUND) for bt in range(X_TILES) for n in range(2)
+            (n, bt, a) for n in range(2) for bt in range(X_TILES) for a in range(PASSES_PER_ROUND)
         ]
         per_run = -(-len(round_matmuls) // RUNS_PER_ROUND)
 
         def multiply_run(i, run):
             codes, scales = mx_tiles[i % MX_BUFS]
-            for a, bt, n in round_matmuls[run * per_run : (run + 1) * per_run]:
+            for n, bt, a in round_matmuls[run * per_run : (run + 1) * per_run]:
                 c = i * PASSES_PER_ROUND + a
                 x_cols = slice(a * COLS + bt * P, a * COLS + (bt + 1) * P)
                 w0 = a * COLS + X_TILES * P + n * N_MOVING
@@ -240,90 +242,110 @@ def tile_share_lstm_cell_pa_k_kernel(
                 nc.vector.tensor_copy(out=addend[:, bt, LSTM_GATES:GATES], in_=shared[:])
 
         for turn in range(N_RUNS + LAG):
-            if turn < N_RUNS:
-                transpose_run(turn // RUNS_PER_ROUND, turn % RUNS_PER_ROUND)
             if 1 <= turn <= N_RUNS:
                 quantise_run((turn - 1) // RUNS_PER_ROUND, (turn - 1) % RUNS_PER_ROUND)
+            if turn < N_RUNS:
+                transpose_run(turn // RUNS_PER_ROUND, turn % RUNS_PER_ROUND)
             if turn >= LAG:
                 multiply_run((turn - LAG) // RUNS_PER_ROUND, (turn - LAG) % RUNS_PER_ROUND)
             if turn == SMALL_PRODUCTS_AFTER_RUN:
                 small_products()
 
-        def block(tile, j):
-            return tile[:, :, j * D_HID : (j + 1) * D_HID]
-
         pre = tail.tile([P, X_TILES, GATES], F32)
         gate = tail.tile([P, X_TILES, GATES], F32)
-        for bt in range(X_TILES):
+
+        def new(name):
+            return tail.tile([P, X_TILES, D_HID], F32, name=name)
+
+        def store(out, tile, bt):
+            nc.sync.dma_start(out=out[bt * P : (bt + 1) * P, :], in_=tile[:, bt, :])
+
+        def gate_block(bt, g):
+            return gate[:, bt, g * D_HID : (g + 1) * D_HID]
+
+        kept, fresh, c_t, tanh_c, tc_m, h = [
+            new(n) for n in ("kept", "fresh", "c_t", "tanh_c", "tc_m", "h")
+        ]
+        b_less_o = [new("b%d_less_o" % j) for j in range(3)]
+        s_0, s_1, s_2, rest_1, rest_2 = [new(n) for n in ("s_0", "s_1", "s_2", "rest_1", "rest_2")]
+
+        def lstm_gates(bt):
             nc.vector.tensor_add(
                 out=pre[:, bt, 0:N_MOVING], in0=acc[bt][0][:], in1=addend[:, bt, 0:N_MOVING]
             )
-        nc.scalar.activation(out=gate[:, :, 0 : 3 * D_HID], in_=pre[:, :, 0 : 3 * D_HID], func=ACT.Sigmoid)
-        nc.scalar.activation(out=block(gate, 3), in_=block(pre, 3), func=ACT.Tanh)
-        for bt in range(X_TILES):
+            nc.scalar.activation(
+                out=gate[:, bt, 0 : 3 * D_HID], in_=pre[:, bt, 0 : 3 * D_HID], func=ACT.Sigmoid
+            )
+            nc.scalar.activation(
+                out=gate_block(bt, 3), in_=pre[:, bt, 3 * D_HID : LSTM_GATES], func=ACT.Tanh
+            )
+
+        def shared_sums(bt):
             nc.vector.tensor_add(
                 out=pre[:, bt, N_MOVING:GATES],
                 in0=acc[bt][1][:, 0 : GATES - N_MOVING],
                 in1=addend[:, bt, N_MOVING:GATES],
             )
-        nc.scalar.activation(
-            out=gate[:, :, LSTM_GATES:GATES], in_=pre[:, :, LSTM_GATES:GATES], func=ACT.Sigmoid
-        )
-        i_g, f_g, o_g, c_hat = [block(gate, j) for j in range(4)]
 
-        kept = tail.tile([P, X_TILES, D_HID], F32)
-        nc.vector.tensor_mul(out=kept[:], in0=f_g, in1=c_masked[:])
-        fresh = tail.tile([P, X_TILES, D_HID], F32)
-        for bt in range(X_TILES):
+        def cell_state(bt):
             nc.vector.scalar_tensor_tensor(
-                out=fresh[:, bt, :], in0=i_g[:, bt, :], scalar=mask_col[:, bt : bt + 1],
-                in1=c_hat[:, bt, :], op0=ALU.mult, op1=ALU.mult,
+                out=fresh[:, bt, :], in0=gate_block(bt, 0), scalar=mask_col[:, bt : bt + 1],
+                in1=gate_block(bt, 3), op0=ALU.mult, op1=ALU.mult,
             )
-        c_t = tail.tile([P, X_TILES, D_HID], F32)
-        nc.vector.tensor_add(out=c_t[:], in0=kept[:], in1=fresh[:])
-        tanh_c = tail.tile([P, X_TILES, D_HID], F32)
-        nc.scalar.activation(out=tanh_c[:], in_=c_t[:], func=ACT.Tanh)
+            nc.vector.tensor_mul(out=kept[:, bt, :], in0=gate_block(bt, 1), in1=c_masked[:, bt, :])
+            nc.vector.tensor_add(out=c_t[:, bt, :], in0=kept[:, bt, :], in1=fresh[:, bt, :])
+            store(out_1, c_t, bt)
+            nc.scalar.activation(
+                out=gate[:, bt, LSTM_GATES:GATES], in_=pre[:, bt, LSTM_GATES:GATES], func=ACT.Sigmoid
+            )
+            nc.scalar.activation(out=tanh_c[:, bt, :], in_=c_t[:, bt, :], func=ACT.Tanh)
 
-        def store(out, tile):
-            nc.sync.dma_start(out=out.rearrange("(t p) d -> p t d", p=P), in_=tile[:])
-
-        store(out_1, c_t)
-        b_less_o = []
-        for j in range(3):
-            diff = tail.tile([P, X_TILES, D_HID], F32, name="b_less_o%d" % j)
-            nc.vector.tensor_sub(out=diff[:], in0=block(gate, 4 + j), in1=o_g)
-            b_less_o.append(diff)
-        tc_m = tail.tile([P, X_TILES, D_HID], F32)
-        for bt in range(X_TILES):
+        def hidden_and_s_0(bt):
+            o_g = gate_block(bt, 2)
+            for j in range(2):
+                nc.vector.tensor_sub(out=b_less_o[j][:, bt, :], in0=gate_block(bt, 4 + j), in1=o_g)
             nc.vector.tensor_scalar_mul(
                 out=tc_m[:, bt, :], in0=tanh_c[:, bt, :], scalar1=mask_col[:, bt : bt + 1]
             )
-        s_0 = tail.tile([P, X_TILES, D_HID], F32)
-        nc.vector.scalar_tensor_tensor(
-            out=s_0[:], in0=b_less_o[0][:], scalar=1.0, in1=tc_m[:], op0=ALU.add, op1=ALU.mult
-        )
-        store(out_2, s_0)
-        h = tail.tile([P, X_TILES, D_HID], F32)
-        nc.vector.tensor_mul(out=h[:], in0=o_g, in1=tc_m[:])
-        store(out_0, h)
-        rest_1 = tail.tile([P, X_TILES, D_HID], F32)
-        nc.vector.scalar_tensor_tensor(
-            out=rest_1[:], in0=b_less_o[1][:], scalar=2.0, in1=s_0[:], op0=ALU.add, op1=ALU.subtract
-        )
-        rest_2 = tail.tile([P, X_TILES, D_HID], F32)
-        nc.vector.scalar_tensor_tensor(
-            out=rest_2[:], in0=s_0[:], scalar=-2.0, in1=b_less_o[2][:], op0=ALU.mult, op1=ALU.add
-        )
-        s_1 = tail.tile([P, X_TILES, D_HID], F32)
-        nc.vector.scalar_tensor_tensor(
-            out=s_1[:], in0=rest_1[:], scalar=0.5, in1=tc_m[:], op0=ALU.mult, op1=ALU.mult
-        )
-        store(out_3, s_1)
-        nc.vector.scalar_tensor_tensor(
-            out=rest_2[:], in0=rest_2[:], scalar=3.0, in1=s_1[:], op0=ALU.add, op1=ALU.subtract
-        )
-        s_2 = tail.tile([P, X_TILES, D_HID], F32)
-        nc.vector.scalar_tensor_tensor(
-            out=s_2[:], in0=rest_2[:], scalar=1.0 / 3.0, in1=tc_m[:], op0=ALU.mult, op1=ALU.mult
-        )
-        store(out_4, s_2)
+            nc.vector.tensor_sub(out=b_less_o[2][:, bt, :], in0=gate_block(bt, 6), in1=o_g)
+            nc.vector.scalar_tensor_tensor(
+                out=s_0[:, bt, :], in0=b_less_o[0][:, bt, :], scalar=1.0, in1=tc_m[:, bt, :],
+                op0=ALU.add, op1=ALU.mult,
+            )
+            store(out_2, s_0, bt)
+            nc.vector.tensor_mul(out=h[:, bt, :], in0=o_g, in1=tc_m[:, bt, :])
+            store(out_0, h, bt)
+
+        def shared_s_1(bt):
+            nc.vector.scalar_tensor_tensor(
+                out=rest_1[:, bt, :], in0=b_less_o[1][:, bt, :], scalar=2.0, in1=s_0[:, bt, :],
+                op0=ALU.add, op1=ALU.subtract,
+            )
+            nc.vector.scalar_tensor_tensor(
+                out=rest_2[:, bt, :], in0=s_0[:, bt, :], scalar=-2.0, in1=b_less_o[2][:, bt, :],
+                op0=ALU.mult, op1=ALU.add,
+            )
+            nc.vector.scalar_tensor_tensor(
+                out=s_1[:, bt, :], in0=rest_1[:, bt, :], scalar=0.5, in1=tc_m[:, bt, :],
+                op0=ALU.mult, op1=ALU.mult,
+            )
+            store(out_3, s_1, bt)
+
+        def rest_of_s_2(bt):
+            nc.vector.scalar_tensor_tensor(
+                out=rest_2[:, bt, :], in0=rest_2[:, bt, :], scalar=3.0, in1=s_1[:, bt, :],
+                op0=ALU.add, op1=ALU.subtract,
+            )
+
+        def shared_s_2(bt):
+            nc.vector.scalar_tensor_tensor(
+                out=s_2[:, bt, :], in0=rest_2[:, bt, :], scalar=1.0 / 3.0, in1=tc_m[:, bt, :],
+                op0=ALU.mult, op1=ALU.mult,
+            )
+            store(out_4, s_2, bt)
+
+        for step in (
+            lstm_gates, shared_sums, cell_state, hidden_and_s_0, shared_s_1, rest_of_s_2, shared_s_2
+        ):
+            for bt in range(X_TILES):
+                step(bt)

@@ -40,8 +40,8 @@ T_BANKS = 4
 RUNS_PER_ROUND = 3
 RUN_TILES = ROW_TILES // RUNS_PER_ROUND
 N_RUNS = ROUNDS * RUNS_PER_ROUND
-RUN_CUTS = ((0, 2 * P), (2 * P, 3 * P))
-LAG = 4
+ROW_CUTS = ((0, 1024), (1024, ROWS))
+LAG = 5
 MX_BUFS = 3
 SMALL_PRODUCTS_AFTER_RUN = 7
 
@@ -146,18 +146,16 @@ def tile_share_lstm_cell_pa_k_kernel(
                         nc.tensor.transpose(bank[:, a, u, :], words[:, w0 : w0 + P], ident_f32[:])
                 dst = grouped_words[:, :, rt * P : (rt + 1) * P, :]
                 src = bank[:].rearrange("p a u r -> p a r u")
-                if rt % RUN_TILES == 1:
+                if rt % RUN_TILES == 1 and run > 0:
                     nc.vector.tensor_copy(out=dst, in_=src)
                 else:
                     nc.scalar.copy(out=dst, in_=src)
                 if r == ROUNDS_PER_SLAB - 1 and s + RAW_SLABS < SLABS:
                     load(s + RAW_SLABS, rt, 0, 1)
 
-        def quantise_run(i, run):
+        def quantise_round(i):
             codes, scales = mx_tiles[i % MX_BUFS]
-            first_row = run * RUN_TILES * P
-            for cut_lo, cut_hi in RUN_CUTS:
-                lo, hi = first_row + cut_lo, first_row + cut_hi
+            for lo, hi in ROW_CUTS:
                 for a in range(PASSES_PER_ROUND):
                     nc.vector.quantize_mx(
                         out=codes[:, a * COLS + lo : a * COLS + hi].bitcast(FP8X4),
@@ -171,13 +169,13 @@ def tile_share_lstm_cell_pa_k_kernel(
         ]
 
         round_matmuls = [
-            (n, bt, a) for n in range(2) for bt in range(X_TILES) for a in range(PASSES_PER_ROUND)
+            (n, a, bt) for n in range(2) for a in range(PASSES_PER_ROUND) for bt in range(X_TILES)
         ]
         per_run = -(-len(round_matmuls) // RUNS_PER_ROUND)
 
         def multiply_run(i, run):
             codes, scales = mx_tiles[i % MX_BUFS]
-            for n, bt, a in round_matmuls[run * per_run : (run + 1) * per_run]:
+            for n, a, bt in round_matmuls[run * per_run : (run + 1) * per_run]:
                 c = i * PASSES_PER_ROUND + a
                 x_cols = slice(a * COLS + bt * P, a * COLS + (bt + 1) * P)
                 w0 = a * COLS + X_TILES * P + n * N_MOVING
@@ -242,110 +240,91 @@ def tile_share_lstm_cell_pa_k_kernel(
                 nc.vector.tensor_copy(out=addend[:, bt, LSTM_GATES:GATES], in_=shared[:])
 
         for turn in range(N_RUNS + LAG):
-            if 1 <= turn <= N_RUNS:
-                quantise_run((turn - 1) // RUNS_PER_ROUND, (turn - 1) % RUNS_PER_ROUND)
             if turn < N_RUNS:
                 transpose_run(turn // RUNS_PER_ROUND, turn % RUNS_PER_ROUND)
+                if turn % RUNS_PER_ROUND == RUNS_PER_ROUND - 1:
+                    quantise_round(turn // RUNS_PER_ROUND)
             if turn >= LAG:
                 multiply_run((turn - LAG) // RUNS_PER_ROUND, (turn - LAG) % RUNS_PER_ROUND)
             if turn == SMALL_PRODUCTS_AFTER_RUN:
                 small_products()
 
+        def block(tile, j):
+            return tile[:, :, j * D_HID : (j + 1) * D_HID]
+
         pre = tail.tile([P, X_TILES, GATES], F32)
         gate = tail.tile([P, X_TILES, GATES], F32)
-
-        def new(name):
-            return tail.tile([P, X_TILES, D_HID], F32, name=name)
-
-        def store(out, tile, bt):
-            nc.sync.dma_start(out=out[bt * P : (bt + 1) * P, :], in_=tile[:, bt, :])
-
-        def gate_block(bt, g):
-            return gate[:, bt, g * D_HID : (g + 1) * D_HID]
-
-        kept, fresh, c_t, tanh_c, tc_m, h = [
-            new(n) for n in ("kept", "fresh", "c_t", "tanh_c", "tc_m", "h")
-        ]
-        b_less_o = [new("b%d_less_o" % j) for j in range(3)]
-        s_0, s_1, s_2, rest_1, rest_2 = [new(n) for n in ("s_0", "s_1", "s_2", "rest_1", "rest_2")]
-
-        def lstm_gates(bt):
+        for bt in range(X_TILES):
             nc.vector.tensor_add(
                 out=pre[:, bt, 0:N_MOVING], in0=acc[bt][0][:], in1=addend[:, bt, 0:N_MOVING]
             )
-            nc.scalar.activation(
-                out=gate[:, bt, 0 : 3 * D_HID], in_=pre[:, bt, 0 : 3 * D_HID], func=ACT.Sigmoid
-            )
-            nc.scalar.activation(
-                out=gate_block(bt, 3), in_=pre[:, bt, 3 * D_HID : LSTM_GATES], func=ACT.Tanh
-            )
-
-        def shared_sums(bt):
+        nc.scalar.activation(out=gate[:, :, 0 : 3 * D_HID], in_=pre[:, :, 0 : 3 * D_HID], func=ACT.Sigmoid)
+        nc.scalar.activation(out=block(gate, 3), in_=block(pre, 3), func=ACT.Tanh)
+        for bt in range(X_TILES):
             nc.vector.tensor_add(
                 out=pre[:, bt, N_MOVING:GATES],
                 in0=acc[bt][1][:, 0 : GATES - N_MOVING],
                 in1=addend[:, bt, N_MOVING:GATES],
             )
+        nc.scalar.activation(
+            out=gate[:, :, LSTM_GATES:GATES], in_=pre[:, :, LSTM_GATES:GATES], func=ACT.Sigmoid
+        )
+        i_g, f_g, o_g, c_hat = [block(gate, j) for j in range(4)]
 
-        def cell_state(bt):
+        kept = tail.tile([P, X_TILES, D_HID], F32)
+        nc.vector.tensor_mul(out=kept[:], in0=f_g, in1=c_masked[:])
+        fresh = tail.tile([P, X_TILES, D_HID], F32)
+        for bt in range(X_TILES):
             nc.vector.scalar_tensor_tensor(
-                out=fresh[:, bt, :], in0=gate_block(bt, 0), scalar=mask_col[:, bt : bt + 1],
-                in1=gate_block(bt, 3), op0=ALU.mult, op1=ALU.mult,
+                out=fresh[:, bt, :], in0=i_g[:, bt, :], scalar=mask_col[:, bt : bt + 1],
+                in1=c_hat[:, bt, :], op0=ALU.mult, op1=ALU.mult,
             )
-            nc.vector.tensor_mul(out=kept[:, bt, :], in0=gate_block(bt, 1), in1=c_masked[:, bt, :])
-            nc.vector.tensor_add(out=c_t[:, bt, :], in0=kept[:, bt, :], in1=fresh[:, bt, :])
-            store(out_1, c_t, bt)
-            nc.scalar.activation(
-                out=gate[:, bt, LSTM_GATES:GATES], in_=pre[:, bt, LSTM_GATES:GATES], func=ACT.Sigmoid
-            )
-            nc.scalar.activation(out=tanh_c[:, bt, :], in_=c_t[:, bt, :], func=ACT.Tanh)
+        c_t = tail.tile([P, X_TILES, D_HID], F32)
+        nc.vector.tensor_add(out=c_t[:], in0=kept[:], in1=fresh[:])
+        tanh_c = tail.tile([P, X_TILES, D_HID], F32)
+        nc.scalar.activation(out=tanh_c[:], in_=c_t[:], func=ACT.Tanh)
 
-        def hidden_and_s_0(bt):
-            o_g = gate_block(bt, 2)
-            for j in range(2):
-                nc.vector.tensor_sub(out=b_less_o[j][:, bt, :], in0=gate_block(bt, 4 + j), in1=o_g)
+        def store(out, tile):
+            nc.sync.dma_start(out=out.rearrange("(t p) d -> p t d", p=P), in_=tile[:])
+
+        store(out_1, c_t)
+        b_less_o = tail.tile([P, X_TILES, 3, D_HID], F32)
+        nc.vector.tensor_sub(
+            out=b_less_o[:],
+            in0=gate[:, :, LSTM_GATES:GATES].rearrange("p t (j d) -> p t j d", j=3),
+            in1=o_g.unsqueeze(2).to_broadcast([P, X_TILES, 3, D_HID]),
+        )
+        tc_m = tail.tile([P, X_TILES, D_HID], F32)
+        for bt in range(X_TILES):
             nc.vector.tensor_scalar_mul(
                 out=tc_m[:, bt, :], in0=tanh_c[:, bt, :], scalar1=mask_col[:, bt : bt + 1]
             )
-            nc.vector.tensor_sub(out=b_less_o[2][:, bt, :], in0=gate_block(bt, 6), in1=o_g)
-            nc.vector.scalar_tensor_tensor(
-                out=s_0[:, bt, :], in0=b_less_o[0][:, bt, :], scalar=1.0, in1=tc_m[:, bt, :],
-                op0=ALU.add, op1=ALU.mult,
-            )
-            store(out_2, s_0, bt)
-            nc.vector.tensor_mul(out=h[:, bt, :], in0=o_g, in1=tc_m[:, bt, :])
-            store(out_0, h, bt)
-
-        def shared_s_1(bt):
-            nc.vector.scalar_tensor_tensor(
-                out=rest_1[:, bt, :], in0=b_less_o[1][:, bt, :], scalar=2.0, in1=s_0[:, bt, :],
-                op0=ALU.add, op1=ALU.subtract,
-            )
-            nc.vector.scalar_tensor_tensor(
-                out=rest_2[:, bt, :], in0=s_0[:, bt, :], scalar=-2.0, in1=b_less_o[2][:, bt, :],
-                op0=ALU.mult, op1=ALU.add,
-            )
-            nc.vector.scalar_tensor_tensor(
-                out=s_1[:, bt, :], in0=rest_1[:, bt, :], scalar=0.5, in1=tc_m[:, bt, :],
-                op0=ALU.mult, op1=ALU.mult,
-            )
-            store(out_3, s_1, bt)
-
-        def rest_of_s_2(bt):
-            nc.vector.scalar_tensor_tensor(
-                out=rest_2[:, bt, :], in0=rest_2[:, bt, :], scalar=3.0, in1=s_1[:, bt, :],
-                op0=ALU.add, op1=ALU.subtract,
-            )
-
-        def shared_s_2(bt):
-            nc.vector.scalar_tensor_tensor(
-                out=s_2[:, bt, :], in0=rest_2[:, bt, :], scalar=1.0 / 3.0, in1=tc_m[:, bt, :],
-                op0=ALU.mult, op1=ALU.mult,
-            )
-            store(out_4, s_2, bt)
-
-        for step in (
-            lstm_gates, shared_sums, cell_state, hidden_and_s_0, shared_s_1, rest_of_s_2, shared_s_2
-        ):
-            for bt in range(X_TILES):
-                step(bt)
+        s_0 = tail.tile([P, X_TILES, D_HID], F32)
+        nc.vector.scalar_tensor_tensor(
+            out=s_0[:], in0=b_less_o[:, :, 0, :], scalar=1.0, in1=tc_m[:], op0=ALU.add, op1=ALU.mult
+        )
+        store(out_2, s_0)
+        h = tail.tile([P, X_TILES, D_HID], F32)
+        nc.vector.tensor_mul(out=h[:], in0=o_g, in1=tc_m[:])
+        store(out_0, h)
+        rest_1 = tail.tile([P, X_TILES, D_HID], F32)
+        nc.vector.scalar_tensor_tensor(
+            out=rest_1[:], in0=b_less_o[:, :, 1, :], scalar=2.0, in1=s_0[:], op0=ALU.add, op1=ALU.subtract
+        )
+        rest_2 = tail.tile([P, X_TILES, D_HID], F32)
+        nc.vector.scalar_tensor_tensor(
+            out=rest_2[:], in0=s_0[:], scalar=-2.0, in1=b_less_o[:, :, 2, :], op0=ALU.mult, op1=ALU.add
+        )
+        s_1 = tail.tile([P, X_TILES, D_HID], F32)
+        nc.vector.scalar_tensor_tensor(
+            out=s_1[:], in0=rest_1[:], scalar=0.5, in1=tc_m[:], op0=ALU.mult, op1=ALU.mult
+        )
+        store(out_3, s_1)
+        nc.vector.scalar_tensor_tensor(
+            out=rest_2[:], in0=rest_2[:], scalar=3.0, in1=s_1[:], op0=ALU.add, op1=ALU.subtract
+        )
+        s_2 = tail.tile([P, X_TILES, D_HID], F32)
+        nc.vector.scalar_tensor_tensor(
+            out=s_2[:], in0=rest_2[:], scalar=1.0 / 3.0, in1=tc_m[:], op0=ALU.mult, op1=ALU.mult
+        )
+        store(out_4, s_2)

from contextlib import ExitStack

import concourse.mybir as mybir
from concourse.masks import make_identity

F32 = mybir.dt.float32
BF16 = mybir.dt.bfloat16
I32 = mybir.dt.int32
U32 = mybir.dt.uint32
U8 = mybir.dt.uint8
FP8X4 = mybir.dt.float8_e4m3fn_x4
ALU = mybir.AluOpType
ACT = mybir.ActivationFunctionType

P = 128
BATCH, D_IN, D_HID = 256, 16384, 128
GATES = 7 * D_HID
LSTM_GATES = 4 * D_HID

PACK = 4
K_PASS = P * PACK
N_PASSES = D_IN // K_PASS
HALVES = 2

X_TILES = BATCH // P
W_TILES = GATES // P
ROW_TILES = X_TILES + W_TILES
ROWS = ROW_TILES * P
N_MOVING = 512
COLS = X_TILES * P + 2 * N_MOVING

PASSES_PER_ROUND = 2
ROUND_K = PASSES_PER_ROUND * K_PASS
ROUNDS = D_IN // ROUND_K
SLAB_K = 2048
ROUNDS_PER_SLAB = SLAB_K // ROUND_K
SLABS = D_IN // SLAB_K
RAW_SLABS = 2
T_BANKS = 4
RUNS_PER_ROUND = 3
RUN_TILES = ROW_TILES // RUNS_PER_ROUND
N_RUNS = ROUNDS * RUNS_PER_ROUND
ROW_CUTS = ((0, 1024), (1024, ROWS))
LAG = 5
MX_BUFS = 3
SMALL_PRODUCTS_AFTER_RUN = 7

FLOPS = 2 * BATCH * GATES * D_IN + 2 * BATCH * GATES * D_HID


def tile_share_lstm_cell_pa_k_kernel(
    tc, x, h_minors, c_minors, s0, s1, s2, mask, weight_ih, bias_ih, weight_hh, bias_hh,
    weight_sh0, bias_sh0, weight_sh1, bias_sh1, weight_sh2, bias_sh2,
    out_0, out_1, out_2, out_3, out_4,
):
    nc = tc.nc
    with ExitStack() as ctx:
        ctx.enter_context(tc.manual_schedule())
        const = ctx.enter_context(tc.tile_pool(name="const", bufs=1))
        raw_pool = ctx.enter_context(tc.tile_pool(name="raw", bufs=RAW_SLABS * ROW_TILES))
        grouped_pool = ctx.enter_context(tc.tile_pool(name="grouped", bufs=2))
        tail = ctx.enter_context(tc.tile_pool(name="tail", bufs=1))
        acc_pool = ctx.enter_context(tc.psum_pool(name="acc", bufs=1))
        bank_pool = ctx.enter_context(tc.psum_pool(name="bank", bufs=T_BANKS))

        raw_of = {}

        def load(s, rt, cut, cuts):
            if cut == 0:
                raw_of[(s, rt)] = raw_pool.tile([P, SLAB_K], BF16, name="raw", tag="raw")
            width = SLAB_K // cuts
            k_cols = slice(s * SLAB_K + cut * width, s * SLAB_K + (cut + 1) * width)
            if rt < X_TILES:
                rows = x[rt * P : (rt + 1) * P, k_cols]
            else:
                rows = weight_ih[(rt - X_TILES) * P : (rt - X_TILES + 1) * P, k_cols]
            nc.sync.dma_start(out=raw_of[(s, rt)][:, cut * width : (cut + 1) * width], in_=rows)

        for cut in range(ROUNDS_PER_SLAB):
            for rt in range(ROW_TILES):
                load(0, rt, cut, ROUNDS_PER_SLAB)
        for s in range(1, RAW_SLABS):
            for rt in range(ROW_TILES):
                load(s, rt, 0, 1)

        ident_f32 = const.tile([P, P], F32)
        make_identity(nc, ident_f32[:])
        ident_bf16 = const.tile([P, P], BF16)
        make_identity(nc, ident_bf16[:])
        ones = const.tile([P, P], BF16)
        nc.vector.memset(ones[:], 1.0)
        warm = const.tile([P, 1], F32)
        nc.vector.memset(warm[:], 0.0)
        nc.scalar.activation(out=warm[:], in_=warm[:], func=ACT.Sigmoid)

        mx_tiles = []
        for n in range(MX_BUFS):
            codes = const.tile([P, PASSES_PER_ROUND * COLS], U32, name="codes%d" % n, align_bytes=64)
            scales = const.tile([P, PASSES_PER_ROUND * COLS], U8, name="scales%d" % n, align_bytes=64)
            for a in range(PASSES_PER_ROUND):
                fill = slice(a * COLS + ROWS, (a + 1) * COLS)
                nc.vector.memset(codes[:, fill].bitcast(I32), 0)
                nc.vector.memset(scales[:, fill].bitcast(I32), 0)
            mx_tiles.append((codes, scales))

        act_raw = const.tile([P, 4, X_TILES, D_HID], BF16)
        for j, act in enumerate((h_minors, s0, s1, s2)):
            nc.gpsimd.dma_start(out=act_raw[:, j, :, :], in_=act.rearrange("(t p) d -> p t d", p=P))
        w_raw = const.tile([P, 8, D_HID], BF16)
        nc.vector.memset(w_raw[:, 7, :], 0.0)
        nc.gpsimd.dma_start(out=w_raw[:, 0:4, :], in_=weight_hh.rearrange("(j p) d -> p j d", p=P))
        for j, w_sh in enumerate((weight_sh0, weight_sh1, weight_sh2)):
            nc.gpsimd.dma_start(out=w_raw[:, 4 + j, :], in_=w_sh)
        nc.gpsimd.dma_start(out=w_raw[0:X_TILES, 7, :], in_=mask.rearrange("(t p) -> t p", p=P))
        bias_rows = const.tile([P, GATES], BF16)
        nc.vector.memset(bias_rows[:], 0.0)
        nc.gpsimd.dma_start(out=bias_rows[0:1, :], in_=bias_ih.rearrange("(o n) -> o n", o=1))
        nc.gpsimd.dma_start(
            out=bias_rows[1:2, 0:LSTM_GATES], in_=bias_hh.rearrange("(o n) -> o n", o=1)
        )
        for j, b_sh in enumerate((bias_sh0, bias_sh1, bias_sh2)):
            cols = slice(LSTM_GATES + j * D_HID, LSTM_GATES + (j + 1) * D_HID)
            nc.gpsimd.dma_start(out=bias_rows[1:2, cols], in_=b_sh.rearrange("(o n) -> o n", o=1))
        c_raw = const.tile([P, X_TILES, D_HID], BF16)
        nc.gpsimd.dma_start(out=c_raw[:], in_=c_minors.rearrange("(t p) d -> p t d", p=P))

        grouped_of = {}

        def transpose_run(i, run):
            s, r = divmod(i, ROUNDS_PER_SLAB)
            first_word = r * ROUND_K // 2
            if run == 0:
                grouped_of[i] = grouped_pool.tile(
                    [P, PASSES_PER_ROUND * ROWS * PACK], BF16,
                    name="grouped", tag="grouped", align_bytes=64,
                )
            grouped_words = grouped_of[i][:].bitcast(F32).rearrange(
                "p (a r u) -> p a r u", a=PASSES_PER_ROUND, u=HALVES
            )
            for rt in range(run * RUN_TILES, (run + 1) * RUN_TILES):
                words = raw_of[(s, rt)][:].bitcast(F32)
                bank = bank_pool.tile([P, PASSES_PER_ROUND, HALVES, P], F32, tag="bank")
                for a in range(PASSES_PER_ROUND):
                    for u in range(HALVES):
                        w0 = first_word + (a * HALVES + u) * P
                        nc.tensor.transpose(bank[:, a, u, :], words[:, w0 : w0 + P], ident_f32[:])
                dst = grouped_words[:, :, rt * P : (rt + 1) * P, :]
                src = bank[:].rearrange("p a u r -> p a r u")
                if rt % RUN_TILES == 1 and run > 0:
                    nc.vector.tensor_copy(out=dst, in_=src)
                else:
                    nc.scalar.copy(out=dst, in_=src)
                if r == ROUNDS_PER_SLAB - 1 and s + RAW_SLABS < SLABS:
                    load(s + RAW_SLABS, rt, 0, 1)

        def quantise_round(i):
            codes, scales = mx_tiles[i % MX_BUFS]
            for lo, hi in ROW_CUTS:
                for a in range(PASSES_PER_ROUND):
                    nc.vector.quantize_mx(
                        out=codes[:, a * COLS + lo : a * COLS + hi].bitcast(FP8X4),
                        scales=scales[:, a * COLS + lo : a * COLS + hi],
                        in_=grouped_of[i][:, (a * ROWS + lo) * PACK : (a * ROWS + hi) * PACK],
                    )

        acc = [
            [acc_pool.tile([P, N_MOVING], F32, name="acc%d%d" % (bt, n)) for n in range(2)]
            for bt in range(X_TILES)
        ]

        round_matmuls = [
            (n, a, bt) for n in range(2) for a in range(PASSES_PER_ROUND) for bt in range(X_TILES)
        ]
        per_run = -(-len(round_matmuls) // RUNS_PER_ROUND)

        def multiply_run(i, run):
            codes, scales = mx_tiles[i % MX_BUFS]
            for n, a, bt in round_matmuls[run * per_run : (run + 1) * per_run]:
                c = i * PASSES_PER_ROUND + a
                x_cols = slice(a * COLS + bt * P, a * COLS + (bt + 1) * P)
                w0 = a * COLS + X_TILES * P + n * N_MOVING
                w_cols = slice(w0, w0 + N_MOVING)
                nc.tensor.matmul_mx(
                    out=acc[bt][n][:],
                    lhsT=codes[:, x_cols].bitcast(FP8X4),
                    lhsT_scale=scales[:, x_cols],
                    rhs=codes[:, w_cols].bitcast(FP8X4),
                    rhs_scale=scales[:, w_cols],
                    start=(c == 0),
                    stop=(c == N_PASSES - 1),
                )

        addend = const.tile([P, X_TILES, GATES], F32)
        mask_col = const.tile([P, X_TILES], F32)
        c_masked = const.tile([P, X_TILES, D_HID], F32)

        def small_products():
            act_t_bank = bank_pool.tile([P, 4 * X_TILES, P], BF16, tag="bank")
            for j in range(4):
                for bt in range(X_TILES):
                    nc.tensor.transpose(
                        act_t_bank[:, j * X_TILES + bt, :], act_raw[:, j, bt, :], ident_bf16[:]
                    )
            act_t = const.tile([P, 4 * X_TILES, P], BF16)
            nc.vector.tensor_copy(out=act_t[:], in_=act_t_bank[:])
            w_t_bank = bank_pool.tile([P, 8 * D_HID], BF16, tag="bank")
            for j in range(8):
                nc.tensor.transpose(
                    w_t_bank[:, j * D_HID : (j + 1) * D_HID], w_raw[:, j, :], ident_bf16[:]
                )
            w_t = const.tile([P, 8 * D_HID], BF16)
            nc.scalar.copy(out=w_t[:], in_=w_t_bank[:])
            nc.vector.tensor_copy(out=mask_col[:], in_=w_t[:, GATES : GATES + X_TILES])
            for bt in range(X_TILES):
                nc.vector.tensor_scalar_mul(
                    out=c_masked[:, bt, :], in0=c_raw[:, bt, :], scalar1=mask_col[:, bt : bt + 1]
                )
            for bt in range(X_TILES):
                lstm = bank_pool.tile([P, LSTM_GATES], F32, tag="bank")
                nc.tensor.matmul(
                    out=lstm[:], lhsT=act_t[:, bt, :], rhs=w_t[:, 0:LSTM_GATES],
                    start=True, stop=False,
                )
                nc.tensor.matmul(
                    out=lstm[:], lhsT=ones[:], rhs=bias_rows[:, 0:LSTM_GATES],
                    start=False, stop=True,
                )
                nc.scalar.copy(out=addend[:, bt, 0:LSTM_GATES], in_=lstm[:])
                shared = bank_pool.tile([P, GATES - LSTM_GATES], F32, tag="bank")
                for j in range(3):
                    cols = slice(LSTM_GATES + j * D_HID, LSTM_GATES + (j + 1) * D_HID)
                    group = shared[:, j * D_HID : (j + 1) * D_HID]
                    nc.tensor.matmul(
                        out=group, lhsT=act_t[:, (1 + j) * X_TILES + bt, :], rhs=w_t[:, cols],
                        start=True, stop=False,
                    )
                    nc.tensor.matmul(
                        out=group, lhsT=ones[:], rhs=bias_rows[:, cols], start=False, stop=True
                    )
                nc.vector.tensor_copy(out=addend[:, bt, LSTM_GATES:GATES], in_=shared[:])

        for turn in range(N_RUNS + LAG):
            if turn < N_RUNS:
                transpose_run(turn // RUNS_PER_ROUND, turn % RUNS_PER_ROUND)
                if turn % RUNS_PER_ROUND == RUNS_PER_ROUND - 1:
                    quantise_round(turn // RUNS_PER_ROUND)
            if turn >= LAG:
                multiply_run((turn - LAG) // RUNS_PER_ROUND, (turn - LAG) % RUNS_PER_ROUND)
            if turn == SMALL_PRODUCTS_AFTER_RUN:
                small_products()

        def block(tile, j):
            return tile[:, :, j * D_HID : (j + 1) * D_HID]

        pre = tail.tile([P, X_TILES, GATES], F32)
        gate = tail.tile([P, X_TILES, GATES], F32)
        for bt in range(X_TILES):
            nc.vector.tensor_add(
                out=pre[:, bt, 0:N_MOVING], in0=acc[bt][0][:], in1=addend[:, bt, 0:N_MOVING]
            )
        nc.scalar.activation(out=gate[:, :, 0 : 3 * D_HID], in_=pre[:, :, 0 : 3 * D_HID], func=ACT.Sigmoid)
        nc.scalar.activation(out=block(gate, 3), in_=block(pre, 3), func=ACT.Tanh)
        for bt in range(X_TILES):
            nc.vector.tensor_add(
                out=pre[:, bt, N_MOVING:GATES],
                in0=acc[bt][1][:, 0 : GATES - N_MOVING],
                in1=addend[:, bt, N_MOVING:GATES],
            )
        nc.scalar.activation(
            out=gate[:, :, LSTM_GATES:GATES], in_=pre[:, :, LSTM_GATES:GATES], func=ACT.Sigmoid
        )
        i_g, f_g, o_g, c_hat = [block(gate, j) for j in range(4)]

        kept = tail.tile([P, X_TILES, D_HID], F32)
        nc.vector.tensor_mul(out=kept[:], in0=f_g, in1=c_masked[:])
        fresh = tail.tile([P, X_TILES, D_HID], F32)
        for bt in range(X_TILES):
            nc.vector.scalar_tensor_tensor(
                out=fresh[:, bt, :], in0=i_g[:, bt, :], scalar=mask_col[:, bt : bt + 1],
                in1=c_hat[:, bt, :], op0=ALU.mult, op1=ALU.mult,
            )
        c_t = tail.tile([P, X_TILES, D_HID], F32)
        nc.vector.tensor_add(out=c_t[:], in0=kept[:], in1=fresh[:])
        tanh_c = tail.tile([P, X_TILES, D_HID], F32)
        nc.scalar.activation(out=tanh_c[:], in_=c_t[:], func=ACT.Tanh)

        def store(out, tile):
            nc.sync.dma_start(out=out.rearrange("(t p) d -> p t d", p=P), in_=tile[:])

        store(out_1, c_t)
        b_less_o = tail.tile([P, X_TILES, 3, D_HID], F32)
        nc.vector.tensor_sub(
            out=b_less_o[:],
            in0=gate[:, :, LSTM_GATES:GATES].rearrange("p t (j d) -> p t j d", j=3),
            in1=o_g.unsqueeze(2).to_broadcast([P, X_TILES, 3, D_HID]),
        )
        tc_m = tail.tile([P, X_TILES, D_HID], F32)
        for bt in range(X_TILES):
            nc.vector.tensor_scalar_mul(
                out=tc_m[:, bt, :], in0=tanh_c[:, bt, :], scalar1=mask_col[:, bt : bt + 1]
            )
        s_0 = tail.tile([P, X_TILES, D_HID], F32)
        nc.vector.scalar_tensor_tensor(
            out=s_0[:], in0=b_less_o[:, :, 0, :], scalar=1.0, in1=tc_m[:], op0=ALU.add, op1=ALU.mult
        )
        store(out_2, s_0)
        h = tail.tile([P, X_TILES, D_HID], F32)
        nc.vector.tensor_mul(out=h[:], in0=o_g, in1=tc_m[:])
        store(out_0, h)
        rest_1 = tail.tile([P, X_TILES, D_HID], F32)
        nc.vector.scalar_tensor_tensor(
            out=rest_1[:], in0=b_less_o[:, :, 1, :], scalar=2.0, in1=s_0[:], op0=ALU.add, op1=ALU.subtract
        )
        rest_2 = tail.tile([P, X_TILES, D_HID], F32)
        nc.vector.scalar_tensor_tensor(
            out=rest_2[:], in0=s_0[:], scalar=-2.0, in1=b_less_o[:, :, 2, :], op0=ALU.mult, op1=ALU.add
        )
        s_1 = tail.tile([P, X_TILES, D_HID], F32)
        nc.vector.scalar_tensor_tensor(
            out=s_1[:], in0=rest_1[:], scalar=0.5, in1=tc_m[:], op0=ALU.mult, op1=ALU.mult
        )
        store(out_3, s_1)
        nc.vector.scalar_tensor_tensor(
            out=rest_2[:], in0=rest_2[:], scalar=3.0, in1=s_1[:], op0=ALU.add, op1=ALU.subtract
        )
        s_2 = tail.tile([P, X_TILES, D_HID], F32)
        nc.vector.scalar_tensor_tensor(
            out=s_2[:], in0=rest_2[:], scalar=1.0 / 3.0, in1=tc_m[:], op0=ALU.mult, op1=ALU.mult
        )
        store(out_4, s_2)
